import numpy as np
import ml_dtypes


def mxq(x, axis, fmt="e4m3"):
    dtype, down = {"e4m3": (ml_dtypes.float8_e4m3fn, 7), "e5m2": (ml_dtypes.float8_e5m2, 14)}[fmt]
    v = np.moveaxis(np.asarray(x, np.float32).astype(ml_dtypes.bfloat16).astype(np.float64), axis, -1)
    blocks = v.reshape(v.shape[:-1] + (-1, 32))
    amax = np.abs(blocks).max(-1, keepdims=True)
    byte = np.maximum(np.where(amax > 0, np.frexp(amax)[1] - 1 + 127, 0) - down, 1)
    scale = np.exp2(byte - 127.0)
    codes = (blocks / scale).astype(np.float32).astype(dtype).astype(np.float64)
    return np.moveaxis((codes * scale).reshape(v.shape), -1, axis)


BF16 = ml_dtypes.bfloat16


def bf(x):
    return np.asarray(x, np.float32).astype(BF16)


def f64(x):
    return np.asarray(x).astype(np.float64)


B, K, N = 128, 1024, 1024


def binarize(v):
    return np.where(v >= 0, 1.0, -1.0)


def setup_inputs():
    return {"x": bf(np.random.standard_normal((B, K)) * 3.0 / np.sqrt(K)),
            "w": bf(np.random.standard_normal((K, N)) * 0.6)}


def reference(x, w):
    w_c = np.clip(f64(w), -1.0, 1.0)
    w_b = binarize(w_c)
    return mxq(f64(x), 1, "e4m3") @ mxq(w_b, 0, "e4m3")

@@ -1,0 +1,128 @@
+import concourse.mybir as mybir
+from concourse.masks import make_identity
+
+BF16 = mybir.dt.bfloat16
+F32 = mybir.dt.float32
+U32 = mybir.dt.uint32
+U8 = mybir.dt.uint8
+FP8X4 = mybir.dt.float8_e4m3fn_x4
+ALU = mybir.AluOpType
+ACT = mybir.ActivationFunctionType
+
+P = 128
+PACK = 4
+K_PASS = P * PACK
+BATCH, K, N = 128, 1024, 1024
+PASSES = K // K_PASS
+LOAD_COLS = 512
+BLOCK = 256
+BLOCKS = N // BLOCK
+RUN = 4
+SCALAR_COLS = 160
+VECTOR_COLS = BLOCK - SCALAR_COLS
+SIGN_SCALE = 2.0**64
+SIGN_BIAS = 2.0**-100
+
+FLOPS = 2 * BATCH * K * N
+
+
+def tile_binlinear_s_kernel(tc, x, w, out):
+    nc = tc.nc
+    with tc.tile_pool(name="keep", bufs=1) as keep, tc.psum_pool(name="psum", bufs=1) as psum:
+        x_rows = keep.tile([BATCH, K], BF16)
+        nc.sync.dma_start(out=x_rows[:], in_=x)
+        w_rows = keep.tile([P, PASSES, PACK, N], BF16)
+        for c in range(PASSES):
+            pass_rows = w[c * K_PASS : (c + 1) * K_PASS, :].rearrange("(p j) n -> p j n", j=PACK)
+            for first in range(0, N, LOAD_COLS):
+                nc.sync.dma_start(
+                    out=w_rows[:, c, :, first : first + LOAD_COLS],
+                    in_=pass_rows[:, :, first : first + LOAD_COLS],
+                )
+
+        identity = keep.tile([P, P], F32)
+        make_identity(nc, identity[:])
+        warm_in = keep.tile([P, 1], F32)
+        warm_out = keep.tile([P, 1], F32)
+        nc.vector.memset(warm_in[:], 1.0)
+        nc.scalar.activation(out=warm_out[:], in_=warm_in[:], func=ACT.Sign)
+
+        x_words = x_rows[:].bitcast(F32).rearrange("b (c p u) -> b c u p", c=PASSES, u=2)
+        x_turned = psum.tile([P, PASSES, 2, BATCH], F32)
+        for c in range(PASSES):
+            for u in range(2):
+                nc.tensor.transpose(x_turned[:, c, u, :], x_words[:, c, u, :], identity[:])
+        x_grouped = keep.tile([P, PASSES, BATCH, PACK], BF16, align_bytes=64)
+        nc.vector.tensor_copy(
+            out=x_grouped[:].bitcast(F32), in_=x_turned[:].rearrange("p c u b -> p c b u")
+        )
+        x_codes = keep.tile([P, PASSES, BATCH], U32, align_bytes=64)
+        x_scales = keep.tile([P, PASSES, BATCH], U8, align_bytes=64)
+        nc.vector.quantize_mx(
+            out=x_codes[:].rearrange("p c b -> p (c b)").bitcast(FP8X4),
+            scales=x_scales[:].rearrange("p c b -> p (c b)"),
+            in_=x_grouped[:].rearrange("p c b t -> p (c b t)"),
+        )
+
+        w_steps = keep.tile([P, PASSES, BLOCKS, PACK, VECTOR_COLS], BF16)
+        w_grouped = keep.tile([P, PASSES, N, PACK], BF16, align_bytes=64)
+        w_codes = keep.tile([P, PASSES, N], U32, align_bytes=64)
+        w_scales = keep.tile([P, PASSES, N], U8, align_bytes=64)
+        out_rows = keep.tile([BATCH, N], F32)
+        sums = [psum.tile([BATCH, BLOCK], F32, name="sums%d" % b) for b in range(BLOCKS)]
+
+        def binarise(c, b):
+            s_cols = slice(b * BLOCK, b * BLOCK + SCALAR_COLS)
+            v_cols = slice(b * BLOCK + SCALAR_COLS, (b + 1) * BLOCK)
+            nc.scalar.activation(
+                out=w_grouped[:, c, s_cols, :].rearrange("p (q i) j -> p q j i", i=RUN),
+                in_=w_rows[:, c, :, s_cols].rearrange("p j (q i) -> p q j i", i=RUN),
+                func=ACT.Sign,
+                scale=SIGN_SCALE,
+                bias=SIGN_BIAS,
+            )
+            nc.vector.tensor_scalar(
+                out=w_steps[:, c, b],
+                in0=w_rows[:, c, :, v_cols],
+                scalar1=0.0,
+                scalar2=2.0,
+                op0=ALU.is_ge,
+                op1=ALU.mult,
+            )
+            nc.vector.tensor_scalar(
+                out=w_grouped[:, c, v_cols, :].rearrange("p (q i) j -> p q j i", i=RUN),
+                in0=w_steps[:, c, b].rearrange("p j (q i) -> p q j i", i=RUN),
+                scalar1=-1.0,
+                scalar2=None,
+                op0=ALU.add,
+            )
+
+        def quantise_and_multiply(c, b):
+            cols = slice(b * BLOCK, (b + 1) * BLOCK)
+            nc.vector.quantize_mx(
+                out=w_codes[:, c, cols].bitcast(FP8X4),
+                scales=w_scales[:, c, cols],
+                in_=w_grouped[:, c, cols, :].rearrange("p n j -> p (n j)"),
+            )
+            nc.tensor.matmul_mx(
+                out=sums[b][:],
+                lhsT=x_codes[:, c, :].bitcast(FP8X4),
+                lhsT_scale=x_scales[:, c, :],
+                rhs=w_codes[:, c, cols].bitcast(FP8X4),
+                rhs_scale=w_scales[:, c, cols],
+                start=(c == 0),
+                stop=(c == PASSES - 1),
+            )
+            if c == PASSES - 1:
+                if b % 2 == 0:
+                    nc.scalar.copy(out=out_rows[:, cols], in_=sums[b][:])
+                else:
+                    nc.vector.tensor_copy(out=out_rows[:, cols], in_=sums[b][:])
+                nc.sync.dma_start(out=out[:, cols], in_=out_rows[:, cols])
+
+        units = [(c, b) for c in range(PASSES) for b in range(BLOCKS)]
+        for i, (c, b) in enumerate(units):
+            binarise(c, b)
+            if i > 0:
+                quantise_and_multiply(*units[i - 1])
+        quantise_and_multiply(*units[-1])

@@ -23,12 +23,18 @@ VECTOR_COLS = BLOCK - SCALAR_COLS
 SIGN_SCALE = 2.0**64
 SIGN_BIAS = 2.0**-100
 
+STORE_LAG = 3
+
 FLOPS = 2 * BATCH * K * N
 
 
 def tile_binlinear_s_kernel(tc, x, w, out):
     nc = tc.nc
-    with tc.tile_pool(name="keep", bufs=1) as keep, tc.psum_pool(name="psum", bufs=1) as psum:
+    with (
+        tc.tile_pool(name="keep", bufs=1) as keep,
+        tc.psum_pool(name="psum", bufs=1) as psum,
+        tc.manual_schedule(),
+    ):
         x_rows = keep.tile([BATCH, K], BF16)
         nc.sync.dma_start(out=x_rows[:], in_=x)
         w_rows = keep.tile([P, PASSES, PACK, N], BF16)
@@ -48,21 +54,26 @@ def tile_binlinear_s_kernel(tc, x, w, out):
         nc.scalar.activation(out=warm_out[:], in_=warm_in[:], func=ACT.Sign)
 
         x_words = x_rows[:].bitcast(F32).rearrange("b (c p u) -> b c u p", c=PASSES, u=2)
-        x_turned = psum.tile([P, PASSES, 2, BATCH], F32)
+        x_turned = [psum.tile([P, 2, BATCH], F32, name="x_turned%d" % c) for c in range(PASSES)]
         for c in range(PASSES):
             for u in range(2):
-                nc.tensor.transpose(x_turned[:, c, u, :], x_words[:, c, u, :], identity[:])
+                nc.tensor.transpose(x_turned[c][:, u, :], x_words[:, c, u, :], identity[:])
         x_grouped = keep.tile([P, PASSES, BATCH, PACK], BF16, align_bytes=64)
+        nc.scalar.copy(
+            out=x_grouped[:, 0].bitcast(F32), in_=x_turned[0][:].rearrange("p u b -> p b u")
+        )
         nc.vector.tensor_copy(
-            out=x_grouped[:].bitcast(F32), in_=x_turned[:].rearrange("p c u b -> p c b u")
+            out=x_grouped[:, 1].bitcast(F32), in_=x_turned[1][:].rearrange("p u b -> p b u")
         )
         x_codes = keep.tile([P, PASSES, BATCH], U32, align_bytes=64)
         x_scales = keep.tile([P, PASSES, BATCH], U8, align_bytes=64)
-        nc.vector.quantize_mx(
-            out=x_codes[:].rearrange("p c b -> p (c b)").bitcast(FP8X4),
-            scales=x_scales[:].rearrange("p c b -> p (c b)"),
-            in_=x_grouped[:].rearrange("p c b t -> p (c b t)"),
-        )
+
+        def quantise_x():
+            nc.vector.quantize_mx(
+                out=x_codes[:].rearrange("p c b -> p (c b)").bitcast(FP8X4),
+                scales=x_scales[:].rearrange("p c b -> p (c b)"),
+                in_=x_grouped[:].rearrange("p c b t -> p (c b t)"),
+            )
 
         w_steps = keep.tile([P, PASSES, BLOCKS, PACK, VECTOR_COLS], BF16)
         w_grouped = keep.tile([P, PASSES, N, PACK], BF16, align_bytes=64)
@@ -71,26 +82,31 @@ def tile_binlinear_s_kernel(tc, x, w, out):
         out_rows = keep.tile([BATCH, N], F32)
         sums = [psum.tile([BATCH, BLOCK], F32, name="sums%d" % b) for b in range(BLOCKS)]
 
-        def binarise(c, b):
-            s_cols = slice(b * BLOCK, b * BLOCK + SCALAR_COLS)
-            v_cols = slice(b * BLOCK + SCALAR_COLS, (b + 1) * BLOCK)
+        def scalar_binarise(c, b):
+            cols = slice(b * BLOCK, b * BLOCK + SCALAR_COLS)
             nc.scalar.activation(
-                out=w_grouped[:, c, s_cols, :].rearrange("p (q i) j -> p q j i", i=RUN),
-                in_=w_rows[:, c, :, s_cols].rearrange("p j (q i) -> p q j i", i=RUN),
+                out=w_grouped[:, c, cols, :].rearrange("p (q i) j -> p q j i", i=RUN),
+                in_=w_rows[:, c, :, cols].rearrange("p j (q i) -> p q j i", i=RUN),
                 func=ACT.Sign,
                 scale=SIGN_SCALE,
                 bias=SIGN_BIAS,
             )
+
+        def vector_compare(c, b):
+            cols = slice(b * BLOCK + SCALAR_COLS, (b + 1) * BLOCK)
             nc.vector.tensor_scalar(
                 out=w_steps[:, c, b],
-                in0=w_rows[:, c, :, v_cols],
+                in0=w_rows[:, c, :, cols],
                 scalar1=0.0,
                 scalar2=2.0,
                 op0=ALU.is_ge,
                 op1=ALU.mult,
             )
+
+        def vector_regroup(c, b):
+            cols = slice(b * BLOCK + SCALAR_COLS, (b + 1) * BLOCK)
             nc.vector.tensor_scalar(
-                out=w_grouped[:, c, v_cols, :].rearrange("p (q i) j -> p q j i", i=RUN),
+                out=w_grouped[:, c, cols, :].rearrange("p (q i) j -> p q j i", i=RUN),
                 in0=w_steps[:, c, b].rearrange("p j (q i) -> p q j i", i=RUN),
                 scalar1=-1.0,
                 scalar2=None,
@@ -113,16 +129,25 @@ def tile_binlinear_s_kernel(tc, x, w, out):
                 start=(c == 0),
                 stop=(c == PASSES - 1),
             )
-            if c == PASSES - 1:
-                if b % 2 == 0:
-                    nc.scalar.copy(out=out_rows[:, cols], in_=sums[b][:])
-                else:
-                    nc.vector.tensor_copy(out=out_rows[:, cols], in_=sums[b][:])
-                nc.sync.dma_start(out=out[:, cols], in_=out_rows[:, cols])
+
+        def store_block(b):
+            cols = slice(b * BLOCK, (b + 1) * BLOCK)
+            if b < BLOCKS // 2:
+                nc.vector.tensor_copy(out=out_rows[:, cols], in_=sums[b][:])
+            else:
+                nc.scalar.copy(out=out_rows[:, cols], in_=sums[b][:])
+            nc.sync.dma_start(out=out[:, cols], in_=out_rows[:, cols])
 
         units = [(c, b) for c in range(PASSES) for b in range(BLOCKS)]
-        for i, (c, b) in enumerate(units):
-            binarise(c, b)
-            if i > 0:
+        for i in range(len(units) + STORE_LAG):
+            if i < len(units):
+                scalar_binarise(*units[i])
+                vector_compare(*units[i])
+            if i == 0:
+                quantise_x()
+            elif i <= len(units):
                 quantise_and_multiply(*units[i - 1])
-        quantise_and_multiply(*units[-1])
+            if i < len(units):
+                vector_regroup(*units[i])
+            if i >= STORE_LAG and units[i - STORE_LAG][0] == PASSES - 1:
+                store_block(units[i - STORE_LAG][1])

@@ -15,15 +15,16 @@ K_PASS = P * PACK
 BATCH, K, N = 128, 1024, 1024
 PASSES = K // K_PASS
 LOAD_COLS = 512
+LOADS = PASSES * (N // LOAD_COLS)
 BLOCK = 256
 BLOCKS = N // BLOCK
 RUN = 4
-SCALAR_COLS = 160
-VECTOR_COLS = BLOCK - SCALAR_COLS
+SCALAR_COLS = 320
+VECTOR_COLS = LOAD_COLS - SCALAR_COLS
 SIGN_SCALE = 2.0**64
 SIGN_BIAS = 2.0**-100
 
-STORE_LAG = 3
+STORE_LAG = 2
 
 FLOPS = 2 * BATCH * K * N
 
@@ -38,13 +39,13 @@ def tile_binlinear_s_kernel(tc, x, w, out):
         x_rows = keep.tile([BATCH, K], BF16)
         nc.sync.dma_start(out=x_rows[:], in_=x)
         w_rows = keep.tile([P, PASSES, PACK, N], BF16)
-        for c in range(PASSES):
+        loads = [(c, first) for c in range(PASSES) for first in range(0, N, LOAD_COLS)]
+        for c, first in loads:
             pass_rows = w[c * K_PASS : (c + 1) * K_PASS, :].rearrange("(p j) n -> p j n", j=PACK)
-            for first in range(0, N, LOAD_COLS):
-                nc.sync.dma_start(
-                    out=w_rows[:, c, :, first : first + LOAD_COLS],
-                    in_=pass_rows[:, :, first : first + LOAD_COLS],
-                )
+            nc.sync.dma_start(
+                out=w_rows[:, c, :, first : first + LOAD_COLS],
+                in_=pass_rows[:, :, first : first + LOAD_COLS],
+            )
 
         identity = keep.tile([P, P], F32)
         make_identity(nc, identity[:])
@@ -75,15 +76,15 @@ def tile_binlinear_s_kernel(tc, x, w, out):
                 in_=x_grouped[:].rearrange("p c b t -> p (c b t)"),
             )
 
-        w_steps = keep.tile([P, PASSES, BLOCKS, PACK, VECTOR_COLS], BF16)
+        w_steps = keep.tile([P, LOADS, PACK, VECTOR_COLS], BF16)
         w_grouped = keep.tile([P, PASSES, N, PACK], BF16, align_bytes=64)
         w_codes = keep.tile([P, PASSES, N], U32, align_bytes=64)
         w_scales = keep.tile([P, PASSES, N], U8, align_bytes=64)
         out_rows = keep.tile([BATCH, N], F32)
         sums = [psum.tile([BATCH, BLOCK], F32, name="sums%d" % b) for b in range(BLOCKS)]
 
-        def scalar_binarise(c, b):
-            cols = slice(b * BLOCK, b * BLOCK + SCALAR_COLS)
+        def scalar_binarise(c, first):
+            cols = slice(first, first + SCALAR_COLS)
             nc.scalar.activation(
                 out=w_grouped[:, c, cols, :].rearrange("p (q i) j -> p q j i", i=RUN),
                 in_=w_rows[:, c, :, cols].rearrange("p j (q i) -> p q j i", i=RUN),
@@ -92,10 +93,10 @@ def tile_binlinear_s_kernel(tc, x, w, out):
                 bias=SIGN_BIAS,
             )
 
-        def vector_compare(c, b):
-            cols = slice(b * BLOCK + SCALAR_COLS, (b + 1) * BLOCK)
+        def vector_compare(k, c, first):
+            cols = slice(first + SCALAR_COLS, first + LOAD_COLS)
             nc.vector.tensor_scalar(
-                out=w_steps[:, c, b],
+                out=w_steps[:, k],
                 in0=w_rows[:, c, :, cols],
                 scalar1=0.0,
                 scalar2=2.0,
@@ -103,51 +104,52 @@ def tile_binlinear_s_kernel(tc, x, w, out):
                 op1=ALU.mult,
             )
 
-        def vector_regroup(c, b):
-            cols = slice(b * BLOCK + SCALAR_COLS, (b + 1) * BLOCK)
+        def vector_regroup(k, c, first):
+            cols = slice(first + SCALAR_COLS, first + LOAD_COLS)
             nc.vector.tensor_scalar(
                 out=w_grouped[:, c, cols, :].rearrange("p (q i) j -> p q j i", i=RUN),
-                in0=w_steps[:, c, b].rearrange("p j (q i) -> p q j i", i=RUN),
+                in0=w_steps[:, k].rearrange("p j (q i) -> p q j i", i=RUN),
                 scalar1=-1.0,
                 scalar2=None,
                 op0=ALU.add,
             )
 
-        def quantise_and_multiply(c, b):
-            cols = slice(b * BLOCK, (b + 1) * BLOCK)
-            nc.vector.quantize_mx(
-                out=w_codes[:, c, cols].bitcast(FP8X4),
-                scales=w_scales[:, c, cols],
-                in_=w_grouped[:, c, cols, :].rearrange("p n j -> p (n j)"),
-            )
-            nc.tensor.matmul_mx(
-                out=sums[b][:],
-                lhsT=x_codes[:, c, :].bitcast(FP8X4),
-                lhsT_scale=x_scales[:, c, :],
-                rhs=w_codes[:, c, cols].bitcast(FP8X4),
-                rhs_scale=w_scales[:, c, cols],
-                start=(c == 0),
-                stop=(c == PASSES - 1),
-            )
+        def quantise_and_multiply(c, first):
+            for b in range(first // BLOCK, (first + LOAD_COLS) // BLOCK):
+                cols = slice(b * BLOCK, (b + 1) * BLOCK)
+                nc.vector.quantize_mx(
+                    out=w_codes[:, c, cols].bitcast(FP8X4),
+                    scales=w_scales[:, c, cols],
+                    in_=w_grouped[:, c, cols, :].rearrange("p n j -> p (n j)"),
+                )
+                nc.tensor.matmul_mx(
+                    out=sums[b][:],
+                    lhsT=x_codes[:, c, :].bitcast(FP8X4),
+                    lhsT_scale=x_scales[:, c, :],
+                    rhs=w_codes[:, c, cols].bitcast(FP8X4),
+                    rhs_scale=w_scales[:, c, cols],
+                    start=(c == 0),
+                    stop=(c == PASSES - 1),
+                )
 
-        def store_block(b):
-            cols = slice(b * BLOCK, (b + 1) * BLOCK)
-            if b < BLOCKS // 2:
-                nc.vector.tensor_copy(out=out_rows[:, cols], in_=sums[b][:])
-            else:
-                nc.scalar.copy(out=out_rows[:, cols], in_=sums[b][:])
-            nc.sync.dma_start(out=out[:, cols], in_=out_rows[:, cols])
+        def store(first):
+            for b in range(first // BLOCK, (first + LOAD_COLS) // BLOCK):
+                cols = slice(b * BLOCK, (b + 1) * BLOCK)
+                if b < BLOCKS - 1:
+                    nc.scalar.copy(out=out_rows[:, cols], in_=sums[b][:])
+                else:
+                    nc.vector.tensor_copy(out=out_rows[:, cols], in_=sums[b][:])
+                nc.sync.dma_start(out=out[:, cols], in_=out_rows[:, cols])
 
-        units = [(c, b) for c in range(PASSES) for b in range(BLOCKS)]
-        for i in range(len(units) + STORE_LAG):
-            if i < len(units):
-                scalar_binarise(*units[i])
-                vector_compare(*units[i])
-            if i == 0:
+        for k in range(LOADS + STORE_LAG):
+            if k < LOADS:
+                scalar_binarise(*loads[k])
+                vector_compare(k, *loads[k])
+            if k == 0:
                 quantise_x()
-            elif i <= len(units):
-                quantise_and_multiply(*units[i - 1])
-            if i < len(units):
-                vector_regroup(*units[i])
-            if i >= STORE_LAG and units[i - STORE_LAG][0] == PASSES - 1:
-                store_block(units[i - STORE_LAG][1])
+            elif k <= LOADS:
+                quantise_and_multiply(*loads[k - 1])
+            if k < LOADS:
+                vector_regroup(k, *loads[k])
+            if k >= STORE_LAG and loads[k - STORE_LAG][0] == PASSES - 1:
+                store(loads[k - STORE_LAG][1])

@@ -19,7 +19,7 @@ LOADS = PASSES * (N // LOAD_COLS)
 BLOCK = 256
 BLOCKS = N // BLOCK
 RUN = 4
-SCALAR_COLS = 320
+SCALAR_COLS = 288
 VECTOR_COLS = LOAD_COLS - SCALAR_COLS
 SIGN_SCALE = 2.0**64
 SIGN_BIAS = 2.0**-100

@@ -14,19 +14,17 @@ PACK = 4
 K_PASS = P * PACK
 BATCH, K, N = 128, 1024, 1024
 PASSES = K // K_PASS
-LOAD_COLS = 512
-LOADS = PASSES * (N // LOAD_COLS)
 BLOCK = 256
 BLOCKS = N // BLOCK
 RUN = 4
-SCALAR_COLS = 288
-VECTOR_COLS = LOAD_COLS - SCALAR_COLS
 SIGN_SCALE = 2.0**64
 SIGN_BIAS = 2.0**-100
-
-STORE_LAG = 2
-
 FLOPS = 2 * BATCH * K * N
+
+UNITS = [(0, 0, 256), (0, 256, 256), (0, 512, 512), (1, 0, 512), (1, 512, 512)]
+X_AFTER = 3
+X_COPY_STEP = 2
+SCALAR_SHARE = (9, 16)
 
 
 def tile_binlinear_s_kernel(tc, x, w, out):
@@ -37,15 +35,14 @@ def tile_binlinear_s_kernel(tc, x, w, out):
         tc.manual_schedule(),
     ):
         x_rows = keep.tile([BATCH, K], BF16)
-        nc.sync.dma_start(out=x_rows[:], in_=x)
-        w_rows = keep.tile([P, PASSES, PACK, N], BF16)
-        loads = [(c, first) for c in range(PASSES) for first in range(0, N, LOAD_COLS)]
-        for c, first in loads:
+        w_rows = []
+        for u, (c, first, cols) in enumerate(UNITS):
+            if u == X_AFTER:
+                nc.sync.dma_start(out=x_rows[:], in_=x)
             pass_rows = w[c * K_PASS : (c + 1) * K_PASS, :].rearrange("(p j) n -> p j n", j=PACK)
-            nc.sync.dma_start(
-                out=w_rows[:, c, :, first : first + LOAD_COLS],
-                in_=pass_rows[:, :, first : first + LOAD_COLS],
-            )
+            piece = keep.tile([P, PACK, cols], BF16, name="w_rows%d" % u)
+            nc.sync.dma_start(out=piece[:], in_=pass_rows[:, :, first : first + cols])
+            w_rows.append(piece)
 
         identity = keep.tile([P, P], F32)
         make_identity(nc, identity[:])
@@ -60,14 +57,16 @@ def tile_binlinear_s_kernel(tc, x, w, out):
             for u in range(2):
                 nc.tensor.transpose(x_turned[c][:, u, :], x_words[:, c, u, :], identity[:])
         x_grouped = keep.tile([P, PASSES, BATCH, PACK], BF16, align_bytes=64)
-        nc.scalar.copy(
-            out=x_grouped[:, 0].bitcast(F32), in_=x_turned[0][:].rearrange("p u b -> p b u")
-        )
-        nc.vector.tensor_copy(
-            out=x_grouped[:, 1].bitcast(F32), in_=x_turned[1][:].rearrange("p u b -> p b u")
-        )
         x_codes = keep.tile([P, PASSES, BATCH], U32, align_bytes=64)
         x_scales = keep.tile([P, PASSES, BATCH], U8, align_bytes=64)
+
+        def copy_x():
+            nc.scalar.copy(
+                out=x_grouped[:, 0].bitcast(F32), in_=x_turned[0][:].rearrange("p u b -> p b u")
+            )
+            nc.vector.tensor_copy(
+                out=x_grouped[:, 1].bitcast(F32), in_=x_turned[1][:].rearrange("p u b -> p b u")
+            )
 
         def quantise_x():
             nc.vector.quantize_mx(
@@ -76,80 +75,104 @@ def tile_binlinear_s_kernel(tc, x, w, out):
                 in_=x_grouped[:].rearrange("p c b t -> p (c b t)"),
             )
 
-        w_steps = keep.tile([P, LOADS, PACK, VECTOR_COLS], BF16)
         w_grouped = keep.tile([P, PASSES, N, PACK], BF16, align_bytes=64)
         w_codes = keep.tile([P, PASSES, N], U32, align_bytes=64)
         w_scales = keep.tile([P, PASSES, N], U8, align_bytes=64)
         out_rows = keep.tile([BATCH, N], F32)
         sums = [psum.tile([BATCH, BLOCK], F32, name="sums%d" % b) for b in range(BLOCKS)]
+        w_steps = []
+        for u, (c, first, cols) in enumerate(UNITS):
+            steps_tile = keep.tile(
+                [P, PACK, cols - cols * SCALAR_SHARE[0] // SCALAR_SHARE[1]], BF16, name="w_steps%d" % u
+            )
+            w_steps.append(steps_tile)
 
-        def scalar_binarise(c, first):
-            cols = slice(first, first + SCALAR_COLS)
+        def split(u):
+            c, first, cols = UNITS[u]
+            middle = first + cols * SCALAR_SHARE[0] // SCALAR_SHARE[1]
+            return c, slice(first, middle), slice(middle, first + cols)
+
+        def scalar_binarise(u):
+            c, cols, rest = split(u)
             nc.scalar.activation(
                 out=w_grouped[:, c, cols, :].rearrange("p (q i) j -> p q j i", i=RUN),
-                in_=w_rows[:, c, :, cols].rearrange("p j (q i) -> p q j i", i=RUN),
+                in_=w_rows[u][:, :, 0 : cols.stop - cols.start].rearrange("p j (q i) -> p q j i", i=RUN),
                 func=ACT.Sign,
                 scale=SIGN_SCALE,
                 bias=SIGN_BIAS,
             )
 
-        def vector_compare(k, c, first):
-            cols = slice(first + SCALAR_COLS, first + LOAD_COLS)
+        def vector_compare(u):
+            c, rest, cols = split(u)
             nc.vector.tensor_scalar(
-                out=w_steps[:, k],
-                in0=w_rows[:, c, :, cols],
+                out=w_steps[u][:],
+                in0=w_rows[u][:, :, rest.stop - rest.start :],
                 scalar1=0.0,
                 scalar2=2.0,
                 op0=ALU.is_ge,
                 op1=ALU.mult,
             )
 
-        def vector_regroup(k, c, first):
-            cols = slice(first + SCALAR_COLS, first + LOAD_COLS)
+        def vector_regroup(u):
+            c, rest, cols = split(u)
             nc.vector.tensor_scalar(
                 out=w_grouped[:, c, cols, :].rearrange("p (q i) j -> p q j i", i=RUN),
-                in0=w_steps[:, k].rearrange("p j (q i) -> p q j i", i=RUN),
+                in0=w_steps[u][:].rearrange("p j (q i) -> p q j i", i=RUN),
                 scalar1=-1.0,
                 scalar2=None,
                 op0=ALU.add,
             )
 
-        def quantise_and_multiply(c, first):
-            for b in range(first // BLOCK, (first + LOAD_COLS) // BLOCK):
-                cols = slice(b * BLOCK, (b + 1) * BLOCK)
-                nc.vector.quantize_mx(
-                    out=w_codes[:, c, cols].bitcast(FP8X4),
-                    scales=w_scales[:, c, cols],
-                    in_=w_grouped[:, c, cols, :].rearrange("p n j -> p (n j)"),
-                )
-                nc.tensor.matmul_mx(
-                    out=sums[b][:],
-                    lhsT=x_codes[:, c, :].bitcast(FP8X4),
-                    lhsT_scale=x_scales[:, c, :],
-                    rhs=w_codes[:, c, cols].bitcast(FP8X4),
-                    rhs_scale=w_scales[:, c, cols],
-                    start=(c == 0),
-                    stop=(c == PASSES - 1),
-                )
+        def quantise(c, b):
+            cols = slice(b * BLOCK, (b + 1) * BLOCK)
+            nc.vector.quantize_mx(
+                out=w_codes[:, c, cols].bitcast(FP8X4),
+                scales=w_scales[:, c, cols],
+                in_=w_grouped[:, c, cols, :].rearrange("p n j -> p (n j)"),
+            )
 
-        def store(first):
-            for b in range(first // BLOCK, (first + LOAD_COLS) // BLOCK):
-                cols = slice(b * BLOCK, (b + 1) * BLOCK)
-                if b < BLOCKS - 1:
-                    nc.scalar.copy(out=out_rows[:, cols], in_=sums[b][:])
-                else:
-                    nc.vector.tensor_copy(out=out_rows[:, cols], in_=sums[b][:])
-                nc.sync.dma_start(out=out[:, cols], in_=out_rows[:, cols])
+        def multiply(c, b):
+            cols = slice(b * BLOCK, (b + 1) * BLOCK)
+            nc.tensor.matmul_mx(
+                out=sums[b][:],
+                lhsT=x_codes[:, c, :].bitcast(FP8X4),
+                lhsT_scale=x_scales[:, c, :],
+                rhs=w_codes[:, c, cols].bitcast(FP8X4),
+                rhs_scale=w_scales[:, c, cols],
+                start=(c == 0),
+                stop=(c == PASSES - 1),
+            )
 
-        for k in range(LOADS + STORE_LAG):
-            if k < LOADS:
-                scalar_binarise(*loads[k])
-                vector_compare(k, *loads[k])
-            if k == 0:
+        def store(b):
+            cols = slice(b * BLOCK, (b + 1) * BLOCK)
+            if b < BLOCKS - 1:
+                nc.scalar.copy(out=out_rows[:, cols], in_=sums[b][:])
+            else:
+                nc.vector.tensor_copy(out=out_rows[:, cols], in_=sums[b][:])
+            nc.sync.dma_start(out=out[:, cols], in_=out_rows[:, cols])
+
+        waiting = []
+        for s in range(len(UNITS) + 1):
+            closed = []
+            if s < len(UNITS):
+                scalar_binarise(s)
+                vector_compare(s)
+            if s == X_COPY_STEP + 1:
                 quantise_x()
-            elif k <= LOADS:
-                quantise_and_multiply(*loads[k - 1])
-            if k < LOADS:
-                vector_regroup(k, *loads[k])
-            if k >= STORE_LAG and loads[k - STORE_LAG][0] == PASSES - 1:
-                store(loads[k - STORE_LAG][1])
+            if s >= 1:
+                c, first, cols = UNITS[s - 1]
+                for b in range(first // BLOCK, (first + cols) // BLOCK):
+                    quantise(c, b)
+                    waiting.append((c, b))
+                    if s > X_COPY_STEP:
+                        for cw, bw in waiting:
+                            multiply(cw, bw)
+                            if cw == PASSES - 1:
+                                closed.append(bw)
+                        waiting.clear()
+            if s < len(UNITS):
+                vector_regroup(s)
+            if s == X_COPY_STEP:
+                copy_x()
+            for b in closed:
+                store(b)

@@ -21,9 +21,9 @@ SIGN_SCALE = 2.0**64
 SIGN_BIAS = 2.0**-100
 FLOPS = 2 * BATCH * K * N
 
-UNITS = [(0, 0, 256), (0, 256, 256), (0, 512, 512), (1, 0, 512), (1, 512, 512)]
-X_AFTER = 3
-X_COPY_STEP = 2
+UNITS = [(0, 0, 512), (0, 512, 512), (1, 0, 512), (1, 512, 512)]
+X_AFTER = 2
+X_COPY_STEP = 1
 SCALAR_SHARE = (9, 16)
 
 

@@ -24,7 +24,7 @@ FLOPS = 2 * BATCH * K * N
 UNITS = [(0, 0, 512), (0, 512, 512), (1, 0, 512), (1, 512, 512)]
 X_AFTER = 2
 X_COPY_STEP = 1
-SCALAR_SHARE = (9, 16)
+SCALAR_SHARE = (10, 16)
 
 
 def tile_binlinear_s_kernel(tc, x, w, out):

@@ -22,9 +22,9 @@ SIGN_BIAS = 2.0**-100
 FLOPS = 2 * BATCH * K * N
 
 UNITS = [(0, 0, 512), (0, 512, 512), (1, 0, 512), (1, 512, 512)]
+SCALAR_PARTS = [[288], [288], [320], [256, 160]]
 X_AFTER = 2
 X_COPY_STEP = 1
-SCALAR_SHARE = (10, 16)
 
 
 def tile_binlinear_s_kernel(tc, x, w, out):
@@ -83,24 +83,29 @@ def tile_binlinear_s_kernel(tc, x, w, out):
         w_steps = []
         for u, (c, first, cols) in enumerate(UNITS):
             steps_tile = keep.tile(
-                [P, PACK, cols - cols * SCALAR_SHARE[0] // SCALAR_SHARE[1]], BF16, name="w_steps%d" % u
+                [P, PACK, cols - sum(SCALAR_PARTS[u])], BF16, name="w_steps%d" % u
             )
             w_steps.append(steps_tile)
 
         def split(u):
             c, first, cols = UNITS[u]
-            middle = first + cols * SCALAR_SHARE[0] // SCALAR_SHARE[1]
+            middle = first + sum(SCALAR_PARTS[u])
             return c, slice(first, middle), slice(middle, first + cols)
 
         def scalar_binarise(u):
             c, cols, rest = split(u)
-            nc.scalar.activation(
-                out=w_grouped[:, c, cols, :].rearrange("p (q i) j -> p q j i", i=RUN),
-                in_=w_rows[u][:, :, 0 : cols.stop - cols.start].rearrange("p j (q i) -> p q j i", i=RUN),
-                func=ACT.Sign,
-                scale=SIGN_SCALE,
-                bias=SIGN_BIAS,
-            )
+            done = 0
+            for part in SCALAR_PARTS[u]:
+                nc.scalar.activation(
+                    out=w_grouped[:, c, cols.start + done : cols.start + done + part, :].rearrange(
+                        "p (q i) j -> p q j i", i=RUN
+                    ),
+                    in_=w_rows[u][:, :, done : done + part].rearrange("p j (q i) -> p q j i", i=RUN),
+                    func=ACT.Sign,
+                    scale=SIGN_SCALE,
+                    bias=SIGN_BIAS,
+                )
+                done += part
 
         def vector_compare(u):
             c, rest, cols = split(u)

@@ -22,7 +22,7 @@ SIGN_BIAS = 2.0**-100
 FLOPS = 2 * BATCH * K * N
 
 UNITS = [(0, 0, 512), (0, 512, 512), (1, 0, 512), (1, 512, 512)]
-SCALAR_PARTS = [[288], [288], [320], [256, 160]]
+SCALAR_PARTS = [[256], [256], [320], [256, 160]]
 X_AFTER = 2
 X_COPY_STEP = 1
 
@@ -34,11 +34,12 @@ def tile_binlinear_s_kernel(tc, x, w, out):
         tc.psum_pool(name="psum", bufs=1) as psum,
         tc.manual_schedule(),
     ):
-        x_rows = keep.tile([BATCH, K], BF16)
+        x_rows = [keep.tile([BATCH, K_PASS], BF16, name="x_rows%d" % c) for c in range(PASSES)]
         w_rows = []
         for u, (c, first, cols) in enumerate(UNITS):
-            if u == X_AFTER:
-                nc.sync.dma_start(out=x_rows[:], in_=x)
+            if u >= X_AFTER:
+                cx = u - X_AFTER
+                nc.sync.dma_start(out=x_rows[cx][:], in_=x[:, cx * K_PASS : (cx + 1) * K_PASS])
             pass_rows = w[c * K_PASS : (c + 1) * K_PASS, :].rearrange("(p j) n -> p j n", j=PACK)
             piece = keep.tile([P, PACK, cols], BF16, name="w_rows%d" % u)
             nc.sync.dma_start(out=piece[:], in_=pass_rows[:, :, first : first + cols])
@@ -51,28 +52,30 @@ def tile_binlinear_s_kernel(tc, x, w, out):
         nc.vector.memset(warm_in[:], 1.0)
         nc.scalar.activation(out=warm_out[:], in_=warm_in[:], func=ACT.Sign)
 
-        x_words = x_rows[:].bitcast(F32).rearrange("b (c p u) -> b c u p", c=PASSES, u=2)
+        x_words = [x_rows[c][:].bitcast(F32).rearrange("b (p u) -> b u p", u=2) for c in range(PASSES)]
         x_turned = [psum.tile([P, 2, BATCH], F32, name="x_turned%d" % c) for c in range(PASSES)]
         for c in range(PASSES):
             for u in range(2):
-                nc.tensor.transpose(x_turned[c][:, u, :], x_words[:, c, u, :], identity[:])
+                nc.tensor.transpose(x_turned[c][:, u, :], x_words[c][:, u, :], identity[:])
         x_grouped = keep.tile([P, PASSES, BATCH, PACK], BF16, align_bytes=64)
         x_codes = keep.tile([P, PASSES, BATCH], U32, align_bytes=64)
         x_scales = keep.tile([P, PASSES, BATCH], U8, align_bytes=64)
 
-        def copy_x():
-            nc.scalar.copy(
-                out=x_grouped[:, 0].bitcast(F32), in_=x_turned[0][:].rearrange("p u b -> p b u")
-            )
-            nc.vector.tensor_copy(
-                out=x_grouped[:, 1].bitcast(F32), in_=x_turned[1][:].rearrange("p u b -> p b u")
-            )
+        def copy_x(c):
+            if c == 0:
+                nc.scalar.copy(
+                    out=x_grouped[:, 0].bitcast(F32), in_=x_turned[0][:].rearrange("p u b -> p b u")
+                )
+            else:
+                nc.vector.tensor_copy(
+                    out=x_grouped[:, 1].bitcast(F32), in_=x_turned[1][:].rearrange("p u b -> p b u")
+                )
 
-        def quantise_x():
+        def quantise_x(c):
             nc.vector.quantize_mx(
-                out=x_codes[:].rearrange("p c b -> p (c b)").bitcast(FP8X4),
-                scales=x_scales[:].rearrange("p c b -> p (c b)"),
-                in_=x_grouped[:].rearrange("p c b t -> p (c b t)"),
+                out=x_codes[:, c, :].bitcast(FP8X4),
+                scales=x_scales[:, c, :],
+                in_=x_grouped[:, c].rearrange("p b t -> p (b t)"),
             )
 
         w_grouped = keep.tile([P, PASSES, N, PACK], BF16, align_bytes=64)
@@ -162,8 +165,8 @@ def tile_binlinear_s_kernel(tc, x, w, out):
             if s < len(UNITS):
                 scalar_binarise(s)
                 vector_compare(s)
-            if s == X_COPY_STEP + 1:
-                quantise_x()
+            if X_COPY_STEP < s <= X_COPY_STEP + PASSES:
+                quantise_x(s - X_COPY_STEP - 1)
             if s >= 1:
                 c, first, cols = UNITS[s - 1]
                 for b in range(first // BLOCK, (first + cols) // BLOCK):
@@ -177,7 +180,7 @@ def tile_binlinear_s_kernel(tc, x, w, out):
                         waiting.clear()
             if s < len(UNITS):
                 vector_regroup(s)
-            if s == X_COPY_STEP:
-                copy_x()
+            if X_COPY_STEP <= s < X_COPY_STEP + PASSES:
+                copy_x(s - X_COPY_STEP)
             for b in closed:
                 store(b)

import concourse.mybir as mybir
from concourse.masks import make_identity

BF16 = mybir.dt.bfloat16
F32 = mybir.dt.float32
U32 = mybir.dt.uint32
U8 = mybir.dt.uint8
FP8X4 = mybir.dt.float8_e4m3fn_x4
ALU = mybir.AluOpType
ACT = mybir.ActivationFunctionType

P = 128
PACK = 4
K_PASS = P * PACK
BATCH, K, N = 128, 1024, 1024
PASSES = K // K_PASS
BLOCK = 256
BLOCKS = N // BLOCK
RUN = 4
SIGN_SCALE = 2.0**64
SIGN_BIAS = 2.0**-100
FLOPS = 2 * BATCH * K * N

UNITS = [(0, 0, 512), (0, 512, 512), (1, 0, 512), (1, 512, 512)]
SCALAR_PARTS = [[256], [256], [320], [256, 160]]
X_AFTER = 2
X_COPY_STEP = 1


def tile_binlinear_s_kernel(tc, x, w, out):
    nc = tc.nc
    with (
        tc.tile_pool(name="keep", bufs=1) as keep,
        tc.psum_pool(name="psum", bufs=1) as psum,
        tc.manual_schedule(),
    ):
        x_rows = [keep.tile([BATCH, K_PASS], BF16, name="x_rows%d" % c) for c in range(PASSES)]
        w_rows = []
        for u, (c, first, cols) in enumerate(UNITS):
            if u >= X_AFTER:
                cx = u - X_AFTER
                nc.sync.dma_start(out=x_rows[cx][:], in_=x[:, cx * K_PASS : (cx + 1) * K_PASS])
            pass_rows = w[c * K_PASS : (c + 1) * K_PASS, :].rearrange("(p j) n -> p j n", j=PACK)
            piece = keep.tile([P, PACK, cols], BF16, name="w_rows%d" % u)
            nc.sync.dma_start(out=piece[:], in_=pass_rows[:, :, first : first + cols])
            w_rows.append(piece)

        identity = keep.tile([P, P], F32)
        make_identity(nc, identity[:])
        warm_in = keep.tile([P, 1], F32)
        warm_out = keep.tile([P, 1], F32)
        nc.vector.memset(warm_in[:], 1.0)
        nc.scalar.activation(out=warm_out[:], in_=warm_in[:], func=ACT.Sign)

        x_words = [x_rows[c][:].bitcast(F32).rearrange("b (p u) -> b u p", u=2) for c in range(PASSES)]
        x_turned = [psum.tile([P, 2, BATCH], F32, name="x_turned%d" % c) for c in range(PASSES)]
        for c in range(PASSES):
            for u in range(2):
                nc.tensor.transpose(x_turned[c][:, u, :], x_words[c][:, u, :], identity[:])
        x_grouped = keep.tile([P, PASSES, BATCH, PACK], BF16, align_bytes=64)
        x_codes = keep.tile([P, PASSES, BATCH], U32, align_bytes=64)
        x_scales = keep.tile([P, PASSES, BATCH], U8, align_bytes=64)

        def copy_x(c):
            if c == 0:
                nc.scalar.copy(
                    out=x_grouped[:, 0].bitcast(F32), in_=x_turned[0][:].rearrange("p u b -> p b u")
                )
            else:
                nc.vector.tensor_copy(
                    out=x_grouped[:, 1].bitcast(F32), in_=x_turned[1][:].rearrange("p u b -> p b u")
                )

        def quantise_x(c):
            nc.vector.quantize_mx(
                out=x_codes[:, c, :].bitcast(FP8X4),
                scales=x_scales[:, c, :],
                in_=x_grouped[:, c].rearrange("p b t -> p (b t)"),
            )

        w_grouped = keep.tile([P, PASSES, N, PACK], BF16, align_bytes=64)
        w_codes = keep.tile([P, PASSES, N], U32, align_bytes=64)
        w_scales = keep.tile([P, PASSES, N], U8, align_bytes=64)
        out_rows = keep.tile([BATCH, N], F32)
        sums = [psum.tile([BATCH, BLOCK], F32, name="sums%d" % b) for b in range(BLOCKS)]
        w_steps = []
        for u, (c, first, cols) in enumerate(UNITS):
            steps_tile = keep.tile(
                [P, PACK, cols - sum(SCALAR_PARTS[u])], BF16, name="w_steps%d" % u
            )
            w_steps.append(steps_tile)

        def split(u):
            c, first, cols = UNITS[u]
            middle = first + sum(SCALAR_PARTS[u])
            return c, slice(first, middle), slice(middle, first + cols)

        def scalar_binarise(u):
            c, cols, rest = split(u)
            done = 0
            for part in SCALAR_PARTS[u]:
                nc.scalar.activation(
                    out=w_grouped[:, c, cols.start + done : cols.start + done + part, :].rearrange(
                        "p (q i) j -> p q j i", i=RUN
                    ),
                    in_=w_rows[u][:, :, done : done + part].rearrange("p j (q i) -> p q j i", i=RUN),
                    func=ACT.Sign,
                    scale=SIGN_SCALE,
                    bias=SIGN_BIAS,
                )
                done += part

        def vector_compare(u):
            c, rest, cols = split(u)
            nc.vector.tensor_scalar(
                out=w_steps[u][:],
                in0=w_rows[u][:, :, rest.stop - rest.start :],
                scalar1=0.0,
                scalar2=2.0,
                op0=ALU.is_ge,
                op1=ALU.mult,
            )

        def vector_regroup(u):
            c, rest, cols = split(u)
            nc.vector.tensor_scalar(
                out=w_grouped[:, c, cols, :].rearrange("p (q i) j -> p q j i", i=RUN),
                in0=w_steps[u][:].rearrange("p j (q i) -> p q j i", i=RUN),
                scalar1=-1.0,
                scalar2=None,
                op0=ALU.add,
            )

        def quantise(c, b):
            cols = slice(b * BLOCK, (b + 1) * BLOCK)
            nc.vector.quantize_mx(
                out=w_codes[:, c, cols].bitcast(FP8X4),
                scales=w_scales[:, c, cols],
                in_=w_grouped[:, c, cols, :].rearrange("p n j -> p (n j)"),
            )

        def multiply(c, b):
            cols = slice(b * BLOCK, (b + 1) * BLOCK)
            nc.tensor.matmul_mx(
                out=sums[b][:],
                lhsT=x_codes[:, c, :].bitcast(FP8X4),
                lhsT_scale=x_scales[:, c, :],
                rhs=w_codes[:, c, cols].bitcast(FP8X4),
                rhs_scale=w_scales[:, c, cols],
                start=(c == 0),
                stop=(c == PASSES - 1),
            )

        def store(b):
            cols = slice(b * BLOCK, (b + 1) * BLOCK)
            if b < BLOCKS - 1:
                nc.scalar.copy(out=out_rows[:, cols], in_=sums[b][:])
            else:
                nc.vector.tensor_copy(out=out_rows[:, cols], in_=sums[b][:])
            nc.sync.dma_start(out=out[:, cols], in_=out_rows[:, cols])

        waiting = []
        for s in range(len(UNITS) + 1):
            closed = []
            if s < len(UNITS):
                scalar_binarise(s)
                vector_compare(s)
            if X_COPY_STEP < s <= X_COPY_STEP + PASSES:
                quantise_x(s - X_COPY_STEP - 1)
            if s >= 1:
                c, first, cols = UNITS[s - 1]
                for b in range(first // BLOCK, (first + cols) // BLOCK):
                    quantise(c, b)
                    waiting.append((c, b))
                    if s > X_COPY_STEP:
                        for cw, bw in waiting:
                            multiply(cw, bw)
                            if cw == PASSES - 1:
                                closed.append(bw)
                        waiting.clear()
            if s < len(UNITS):
                vector_regroup(s)
            if X_COPY_STEP <= s < X_COPY_STEP + PASSES:
                copy_x(s - X_COPY_STEP)
            for b in closed:
                store(b)
